import numpy as np
import ml_dtypes


def mxq(x, axis, fmt="e4m3"):
    dtype, down = {"e4m3": (ml_dtypes.float8_e4m3fn, 7), "e5m2": (ml_dtypes.float8_e5m2, 14)}[fmt]
    v = np.moveaxis(np.asarray(x, np.float32).astype(ml_dtypes.bfloat16).astype(np.float64), axis, -1)
    blocks = v.reshape(v.shape[:-1] + (-1, 32))
    amax = np.abs(blocks).max(-1, keepdims=True)
    byte = np.maximum(np.where(amax > 0, np.frexp(amax)[1] - 1 + 127, 0) - down, 1)
    scale = np.exp2(byte - 127.0)
    codes = (blocks / scale).astype(np.float32).astype(dtype).astype(np.float64)
    return np.moveaxis((codes * scale).reshape(v.shape), -1, axis)


WIDE = False


def mx_kscale(k):
    if not WIDE:
        return np.ones(k)
    levels = np.array([10, -10, 5, -5, 0])
    a = np.random.permutation(np.resize(levels, k // 512 * 4)).reshape(k // 512, 4)
    idx = np.arange(k)
    return np.exp2(a[idx // 512, idx % 128 // 32])


BF16 = ml_dtypes.bfloat16


def bf(x):
    return np.asarray(x, np.float32).astype(BF16)


def f64(x):
    return np.asarray(x).astype(np.float64)


M, K, N = 8192, 1024, 256


def setup_inputs():
    bound = np.sqrt(6.0 / (K + N))
    s = mx_kscale(K)
    keep = (s <= 4.0 * s.min()).astype(np.float64)
    return {"x": bf(np.random.standard_normal((M, K)) * (s / s.min())[None, :]),
            "weight": bf(np.random.uniform(-bound, bound, (N, K)) * (keep / keep.mean())[None, :])}


def reference(x, weight):
    w = f64(weight)
    scale = np.mean(np.abs(w))
    binary_no_grad = scale * np.sign(w)
    clipped = np.clip(w, -1.0, 1.0)
    binary_weights = binary_no_grad - clipped + clipped
    return mxq(f64(x), 1, "e4m3") @ mxq(binary_weights, 1, "e4m3").T

@@ -1,0 +1,180 @@
+from contextlib import ExitStack
+
+import concourse.mybir as mybir
+from concourse.masks import make_identity
+
+F32 = mybir.dt.float32
+BF16 = mybir.dt.bfloat16
+U32 = mybir.dt.uint32
+U8 = mybir.dt.uint8
+FP8X4 = mybir.dt.float8_e4m3fn_x4
+ALU = mybir.AluOpType
+ACT = mybir.ActivationFunctionType
+AX = mybir.AxisListType
+
+M, K, N = 8192, 1024, 256
+FLOPS = 2 * M * K * N
+P = 128
+T = 8
+CHUNKS = M // (P * T)
+GROUPS = 2 * CHUNKS
+
+
+def tile_classlayer_t_kernel(tc, x, weight, out):
+    nc = tc.nc
+    xv = x.rearrange("(c p t) k -> c p t k", p=P, t=T)
+    ov = out.rearrange("(c p t) n -> c p t n", p=P, t=T)
+    with ExitStack() as ctx:
+        const = ctx.enter_context(tc.tile_pool(name="const", bufs=1))
+        big = ctx.enter_context(tc.tile_pool(name="big", bufs=5))
+        o_pool = ctx.enter_context(tc.tile_pool(name="outs", bufs=CHUNKS))
+        grp_pool = ctx.enter_context(tc.tile_pool(name="grp", bufs=3))
+        code_pool = ctx.enter_context(tc.tile_pool(name="code", bufs=4))
+        xt_pool = ctx.enter_context(tc.psum_pool(name="xtp", bufs=4))
+        acc_pool = ctx.enter_context(tc.psum_pool(name="accp", bufs=4))
+        ctx.enter_context(tc.manual_schedule())
+
+        ident = const.tile([P, P], F32, name="ident")
+        make_identity(nc, ident[:])
+        ones = const.tile([P, P], F32, name="ones")
+        nc.vector.memset(ones[:], 1.0 / (N * K))
+
+        w_sb = const.tile([P, 2, K], BF16, name="w_sb")
+        for h in range(2):
+            nc.sync.dma_start(out=w_sb[:, h, :], in_=weight[P * h:P * (h + 1), :])
+        xs = []
+        for c in range(CHUNKS):
+            xs.append(big.tile([P, T, K], BF16, tag="xo", name="x%d" % c))
+        cuts = {0: [(0, 2), (2, 4), (4, 8)], 1: [(0, 4), (4, 8)]}
+        for c in range(CHUNKS):
+            for (a, b) in cuts.get(c, [(0, 8)]):
+                nc.sync.dma_start(out=xs[c][:, a:b, :], in_=xv[c][:, a:b, :])
+
+        junk = const.tile([P, 2, K], BF16, name="junk")
+        absum = const.tile([P, 2], F32, name="absum")
+        neg = const.tile([P, 2, K], BF16, name="neg")
+        pos = const.tile([P, 2, K], BF16, name="pos")
+        sgn = const.tile([P, 2, K], BF16, name="sgn")
+        for h in range(2):
+            nc.scalar.activation(out=junk[:, h, :], in_=w_sb[:, h, :], func=ACT.Abs,
+                                 accum_out=absum[:, h:h + 1])
+            nc.vector.tensor_single_scalar(out=neg[:, h, :], in_=w_sb[:, h, :], scalar=0.0, op=ALU.is_lt)
+            nc.vector.tensor_single_scalar(out=pos[:, h, :], in_=w_sb[:, h, :], scalar=0.0, op=ALU.is_gt)
+            nc.vector.tensor_tensor(out=sgn[:, h, :], in0=pos[:, h, :], in1=neg[:, h, :], op=ALU.subtract)
+        sgn_w = sgn[:].bitcast(F32)
+
+        gwt = const.tile([P, 2, N, 4], BF16, name="gwt", align_bytes=64)
+        wcodes = const.tile([P, 2 * N], U32, name="wcodes", align_bytes=64)
+        wscales = const.tile([P, 2 * N], U8, name="wscales", align_bytes=64)
+        scale = const.tile([P, 1], F32, name="scale")
+
+        state = {}
+
+        def transposes(i, mts):
+            c, hf = divmod(i, 2)
+            xw = xs[c][:].bitcast(F32)
+            for mt in mts:
+                xt = xt_pool.tile([P, 4, P], F32, tag="xt", name="xt")
+                for j in range(4):
+                    nc.tensor.transpose(xt[:, j, :], xw[:, 4 * hf + mt, P * j:P * (j + 1)], ident[:])
+                state[("xt", i, mt)] = xt
+
+        def copies(i, mts):
+            if ("grp", i) not in state:
+                state[("grp", i)] = grp_pool.tile([P, 4096], BF16, tag="grp", name="grp", align_bytes=64)
+            gw = state[("grp", i)][:].bitcast(F32)
+            for mt in mts:
+                nc.scalar.copy(
+                    out=gw[:, 512 * mt:512 * (mt + 1)].rearrange("p (g m u) -> p g m u", g=2, u=2),
+                    in_=state[("xt", i, mt)][:].rearrange("p (g u) m -> p g m u", u=2),
+                )
+
+        def quantise(i, a):
+            if ("codes", i) not in state:
+                state[("codes", i)] = code_pool.tile([P, 1024], U32, tag="codes", name="codes", align_bytes=64)
+                state[("scales", i)] = code_pool.tile([P, 1024], U8, tag="scales", name="scales", align_bytes=64)
+            nc.vector.quantize_mx(
+                out=state[("codes", i)][:, 512 * a:512 * (a + 1)].bitcast(FP8X4),
+                scales=state[("scales", i)][:, 512 * a:512 * (a + 1)],
+                in_=state[("grp", i)][:, 2048 * a:2048 * (a + 1)],
+            )
+
+        def passes(i):
+            codes = state[("codes", i)]
+            scales = state[("scales", i)]
+            for b in range(2):
+                acc = acc_pool.tile([P, 512], F32, tag="acc", name="acc")
+                for s in range(2):
+                    for g in range(2):
+                        col = (2 * (2 * b + s) + g) * P
+                        nc.tensor.matmul_mx(
+                            out=acc[:, N * s:N * (s + 1)],
+                            lhsT=codes[:, col:col + P].bitcast(FP8X4),
+                            lhsT_scale=scales[:, col:col + P],
+                            rhs=wcodes[:, N * g:N * (g + 1)].bitcast(FP8X4),
+                            rhs_scale=wscales[:, N * g:N * (g + 1)],
+                            start=(g == 0),
+                            stop=(g == 1),
+                        )
+                state[("acc", i, b)] = acc
+
+        def leave(i, b):
+            c, hf = divmod(i, 2)
+            if ("o", c) not in state:
+                state[("o", c)] = o_pool.tile([P, T, N], F32, tag="o", name="o%d" % c)
+            t0 = 4 * hf + 2 * b
+            nc.vector.tensor_copy(
+                out=state[("o", c)][:, t0:t0 + 2, :].rearrange("p t n -> p (t n)"),
+                in_=state[("acc", i, b)][:],
+            )
+
+        def store(i):
+            c, hf = divmod(i, 2)
+            if c == CHUNKS - 1:
+                nc.sync.dma_start(out=ov[c][:, 4 * hf:4 * hf + 4, :], in_=state[("o", c)][:, 4 * hf:4 * hf + 4, :])
+            elif hf == 1:
+                nc.sync.dma_start(out=ov[c], in_=state[("o", c)][:])
+
+        def w_transposes(h):
+            wt = acc_pool.tile([P, 4, P], F32, tag="acc", name="wt")
+            for j in range(4):
+                nc.tensor.transpose(wt[:, j, :], sgn_w[:, h, P * j:P * (j + 1)], ident[:])
+            state[("wt", h)] = wt
+
+        def w_scaled(h, g):
+            src = state[("wt", h)][:].bitcast(BF16).rearrange("p (g u) (n e) -> p g n u e", u=2, e=2)[:, g]
+            dst = gwt[:, g, P * h:P * (h + 1), :].rearrange("p n (u e) -> p n u e", e=2)
+            if h == 0:
+                nc.vector.tensor_scalar(out=dst, in0=src, scalar1=scale[:, 0:1], scalar2=None, op0=ALU.mult)
+            else:
+                nc.scalar.activation(out=dst, in_=src, func=ACT.Copy, scale=scale[:, 0:1])
+
+        transposes(0, [0, 1])
+        w_transposes(0)
+        transposes(0, [2, 3])
+        w_transposes(1)
+        sm = acc_pool.tile([P, 2], F32, tag="acc", name="sm")
+        nc.tensor.matmul(out=sm[:], lhsT=ones[:], rhs=absum[:], start=True, stop=True)
+        copies(0, [0, 1, 2, 3])
+        quantise(0, 0)
+        nc.vector.tensor_reduce(out=scale[:], in_=sm[:], axis=AX.X, op=ALU.add)
+        for g in range(2):
+            w_scaled(0, g)
+            w_scaled(1, g)
+        nc.vector.quantize_mx(out=wcodes[:].bitcast(FP8X4), scales=wscales[:],
+                              in_=gwt[:].rearrange("p g n t -> p (g n t)"))
+        quantise(0, 1)
+
+        for i in range(1, GROUPS):
+            transposes(i, [0, 1, 2, 3])
+            copies(i, [0, 1, 2, 3])
+            passes(i - 1)
+            quantise(i, 0)
+            leave(i - 1, 0)
+            quantise(i, 1)
+            leave(i - 1, 1)
+            store(i - 1)
+        passes(GROUPS - 1)
+        leave(GROUPS - 1, 0)
+        leave(GROUPS - 1, 1)
+        store(GROUPS - 1)

@@ -15,9 +15,10 @@ AX = mybir.AxisListType
 M, K, N = 8192, 1024, 256
 FLOPS = 2 * M * K * N
 P = 128
-T = 8
+T = 16
 CHUNKS = M // (P * T)
-GROUPS = 2 * CHUNKS
+PER = T // 4
+GROUPS = PER * CHUNKS
 
 
 def tile_classlayer_t_kernel(tc, x, weight, out):
@@ -26,10 +27,10 @@ def tile_classlayer_t_kernel(tc, x, weight, out):
     ov = out.rearrange("(c p t) n -> c p t n", p=P, t=T)
     with ExitStack() as ctx:
         const = ctx.enter_context(tc.tile_pool(name="const", bufs=1))
-        big = ctx.enter_context(tc.tile_pool(name="big", bufs=5))
+        big = ctx.enter_context(tc.tile_pool(name="big", bufs=3))
         o_pool = ctx.enter_context(tc.tile_pool(name="outs", bufs=CHUNKS))
         grp_pool = ctx.enter_context(tc.tile_pool(name="grp", bufs=3))
-        code_pool = ctx.enter_context(tc.tile_pool(name="code", bufs=4))
+        code_pool = ctx.enter_context(tc.tile_pool(name="code", bufs=3))
         xt_pool = ctx.enter_context(tc.psum_pool(name="xtp", bufs=4))
         acc_pool = ctx.enter_context(tc.psum_pool(name="accp", bufs=4))
         ctx.enter_context(tc.manual_schedule())
@@ -45,9 +46,9 @@ def tile_classlayer_t_kernel(tc, x, weight, out):
         xs = []
         for c in range(CHUNKS):
             xs.append(big.tile([P, T, K], BF16, tag="xo", name="x%d" % c))
-        cuts = {0: [(0, 2), (2, 4), (4, 8)], 1: [(0, 4), (4, 8)]}
+        cuts = {0: [(0, 2), (2, 4), (4, 8), (8, 12), (12, 16)], 1: [(0, 8), (8, 16)]}
         for c in range(CHUNKS):
-            for (a, b) in cuts.get(c, [(0, 8)]):
+            for (a, b) in cuts.get(c, [(0, T)]):
                 nc.sync.dma_start(out=xs[c][:, a:b, :], in_=xv[c][:, a:b, :])
 
         junk = const.tile([P, 2, K], BF16, name="junk")
@@ -71,7 +72,7 @@ def tile_classlayer_t_kernel(tc, x, weight, out):
         state = {}
 
         def transposes(i, mts):
-            c, hf = divmod(i, 2)
+            c, hf = divmod(i, PER)
             xw = xs[c][:].bitcast(F32)
             for mt in mts:
                 xt = xt_pool.tile([P, 4, P], F32, tag="xt", name="xt")
@@ -119,7 +120,7 @@ def tile_classlayer_t_kernel(tc, x, weight, out):
                 state[("acc", i, b)] = acc
 
         def leave(i, b):
-            c, hf = divmod(i, 2)
+            c, hf = divmod(i, PER)
             if ("o", c) not in state:
                 state[("o", c)] = o_pool.tile([P, T, N], F32, tag="o", name="o%d" % c)
             t0 = 4 * hf + 2 * b
@@ -129,11 +130,14 @@ def tile_classlayer_t_kernel(tc, x, weight, out):
             )
 
         def store(i):
-            c, hf = divmod(i, 2)
+            c, hf = divmod(i, PER)
             if c == CHUNKS - 1:
-                nc.sync.dma_start(out=ov[c][:, 4 * hf:4 * hf + 4, :], in_=state[("o", c)][:, 4 * hf:4 * hf + 4, :])
-            elif hf == 1:
-                nc.sync.dma_start(out=ov[c], in_=state[("o", c)][:])
+                span = {1: (0, 8), 2: (8, 12), 3: (12, 16)}.get(hf)
+            else:
+                span = {PER - 1: (0, T)}.get(hf)
+            if span is not None:
+                a, b = span
+                nc.sync.dma_start(out=ov[c][:, a:b, :], in_=state[("o", c)][:, a:b, :])
 
         def w_transposes(h):
             wt = acc_pool.tile([P, 4, P], F32, tag="acc", name="wt")

@@ -15,10 +15,9 @@ AX = mybir.AxisListType
 M, K, N = 8192, 1024, 256
 FLOPS = 2 * M * K * N
 P = 128
-T = 16
+T = 8
 CHUNKS = M // (P * T)
-PER = T // 4
-GROUPS = PER * CHUNKS
+GROUPS = 2 * CHUNKS
 
 
 def tile_classlayer_t_kernel(tc, x, weight, out):
@@ -27,10 +26,10 @@ def tile_classlayer_t_kernel(tc, x, weight, out):
     ov = out.rearrange("(c p t) n -> c p t n", p=P, t=T)
     with ExitStack() as ctx:
         const = ctx.enter_context(tc.tile_pool(name="const", bufs=1))
-        big = ctx.enter_context(tc.tile_pool(name="big", bufs=3))
+        big = ctx.enter_context(tc.tile_pool(name="big", bufs=5))
         o_pool = ctx.enter_context(tc.tile_pool(name="outs", bufs=CHUNKS))
         grp_pool = ctx.enter_context(tc.tile_pool(name="grp", bufs=3))
-        code_pool = ctx.enter_context(tc.tile_pool(name="code", bufs=3))
+        code_pool = ctx.enter_context(tc.tile_pool(name="code", bufs=4))
         xt_pool = ctx.enter_context(tc.psum_pool(name="xtp", bufs=4))
         acc_pool = ctx.enter_context(tc.psum_pool(name="accp", bufs=4))
         ctx.enter_context(tc.manual_schedule())
@@ -46,9 +45,9 @@ def tile_classlayer_t_kernel(tc, x, weight, out):
         xs = []
         for c in range(CHUNKS):
             xs.append(big.tile([P, T, K], BF16, tag="xo", name="x%d" % c))
-        cuts = {0: [(0, 2), (2, 4), (4, 8), (8, 12), (12, 16)], 1: [(0, 8), (8, 16)]}
+        cuts = {0: [(0, 2), (2, 4), (4, 8)], 1: [(0, 4), (4, 8)]}
         for c in range(CHUNKS):
-            for (a, b) in cuts.get(c, [(0, T)]):
+            for (a, b) in cuts.get(c, [(0, 8)]):
                 nc.sync.dma_start(out=xs[c][:, a:b, :], in_=xv[c][:, a:b, :])
 
         junk = const.tile([P, 2, K], BF16, name="junk")
@@ -72,7 +71,7 @@ def tile_classlayer_t_kernel(tc, x, weight, out):
         state = {}
 
         def transposes(i, mts):
-            c, hf = divmod(i, PER)
+            c, hf = divmod(i, 2)
             xw = xs[c][:].bitcast(F32)
             for mt in mts:
                 xt = xt_pool.tile([P, 4, P], F32, tag="xt", name="xt")
@@ -80,15 +79,17 @@ def tile_classlayer_t_kernel(tc, x, weight, out):
                     nc.tensor.transpose(xt[:, j, :], xw[:, 4 * hf + mt, P * j:P * (j + 1)], ident[:])
                 state[("xt", i, mt)] = xt
 
-        def copies(i, mts):
+        def copies(i, mts, eng=None):
             if ("grp", i) not in state:
                 state[("grp", i)] = grp_pool.tile([P, 4096], BF16, tag="grp", name="grp", align_bytes=64)
             gw = state[("grp", i)][:].bitcast(F32)
             for mt in mts:
-                nc.scalar.copy(
-                    out=gw[:, 512 * mt:512 * (mt + 1)].rearrange("p (g m u) -> p g m u", g=2, u=2),
-                    in_=state[("xt", i, mt)][:].rearrange("p (g u) m -> p g m u", u=2),
-                )
+                dst = gw[:, 512 * mt:512 * (mt + 1)].rearrange("p (g m u) -> p g m u", g=2, u=2)
+                src = state[("xt", i, mt)][:].rearrange("p (g u) m -> p g m u", u=2)
+                if eng == "v":
+                    nc.vector.tensor_copy(out=dst, in_=src)
+                else:
+                    nc.scalar.copy(out=dst, in_=src)
 
         def quantise(i, a):
             if ("codes", i) not in state:
@@ -119,25 +120,24 @@ def tile_classlayer_t_kernel(tc, x, weight, out):
                         )
                 state[("acc", i, b)] = acc
 
-        def leave(i, b):
-            c, hf = divmod(i, PER)
+        def leave(i, b, eng=None):
+            c, hf = divmod(i, 2)
             if ("o", c) not in state:
                 state[("o", c)] = o_pool.tile([P, T, N], F32, tag="o", name="o%d" % c)
             t0 = 4 * hf + 2 * b
-            nc.vector.tensor_copy(
-                out=state[("o", c)][:, t0:t0 + 2, :].rearrange("p t n -> p (t n)"),
-                in_=state[("acc", i, b)][:],
-            )
+            dst = state[("o", c)][:, t0:t0 + 2, :].rearrange("p t n -> p (t n)")
+            if eng == "s":
+                nc.scalar.copy(out=dst, in_=state[("acc", i, b)][:])
+            else:
+                nc.vector.tensor_copy(out=dst, in_=state[("acc", i, b)][:])
+
+        def store_rows(c, a, b):
+            nc.sync.dma_start(out=ov[c][:, a:b, :], in_=state[("o", c)][:, a:b, :])
 
         def store(i):
-            c, hf = divmod(i, PER)
-            if c == CHUNKS - 1:
-                span = {1: (0, 8), 2: (8, 12), 3: (12, 16)}.get(hf)
-            else:
-                span = {PER - 1: (0, T)}.get(hf)
-            if span is not None:
-                a, b = span
-                nc.sync.dma_start(out=ov[c][:, a:b, :], in_=state[("o", c)][:, a:b, :])
+            c, hf = divmod(i, 2)
+            if hf == 1:
+                store_rows(c, 0, T)
 
         def w_transposes(h):
             wt = acc_pool.tile([P, 4, P], F32, tag="acc", name="wt")
@@ -153,23 +153,24 @@ def tile_classlayer_t_kernel(tc, x, weight, out):
             else:
                 nc.scalar.activation(out=dst, in_=src, func=ACT.Copy, scale=scale[:, 0:1])
 
-        transposes(0, [0, 1])
         w_transposes(0)
-        transposes(0, [2, 3])
-        w_transposes(1)
+        transposes(0, [0, 1])
         sm = acc_pool.tile([P, 2], F32, tag="acc", name="sm")
         nc.tensor.matmul(out=sm[:], lhsT=ones[:], rhs=absum[:], start=True, stop=True)
-        copies(0, [0, 1, 2, 3])
-        quantise(0, 0)
+        w_transposes(1)
+        transposes(0, [2, 3])
+        copies(0, [0, 1])
         nc.vector.tensor_reduce(out=scale[:], in_=sm[:], axis=AX.X, op=ALU.add)
         for g in range(2):
             w_scaled(0, g)
             w_scaled(1, g)
         nc.vector.quantize_mx(out=wcodes[:].bitcast(FP8X4), scales=wscales[:],
                               in_=gwt[:].rearrange("p g n t -> p (g n t)"))
+        copies(0, [2, 3])
+        quantise(0, 0)
         quantise(0, 1)
 
-        for i in range(1, GROUPS):
+        for i in range(1, GROUPS - 1):
             transposes(i, [0, 1, 2, 3])
             copies(i, [0, 1, 2, 3])
             passes(i - 1)
@@ -178,7 +179,20 @@ def tile_classlayer_t_kernel(tc, x, weight, out):
             quantise(i, 1)
             leave(i - 1, 1)
             store(i - 1)
-        passes(GROUPS - 1)
-        leave(GROUPS - 1, 0)
-        leave(GROUPS - 1, 1)
-        store(GROUPS - 1)
+
+        last = GROUPS - 1
+        transposes(last, [0, 1, 2, 3])
+        copies(last, [0, 1])
+        copies(last, [2], "v")
+        copies(last, [3])
+        passes(last - 1)
+        quantise(last, 0)
+        quantise(last, 1)
+        leave(last - 1, 0, "s")
+        leave(last - 1, 1, "s")
+        store_rows(CHUNKS - 1, 0, 4)
+        passes(last)
+        leave(last, 0, "s")
+        store_rows(CHUNKS - 1, 4, 6)
+        leave(last, 1)
+        store_rows(CHUNKS - 1, 6, 8)

@@ -15,9 +15,10 @@ AX = mybir.AxisListType
 M, K, N = 8192, 1024, 256
 FLOPS = 2 * M * K * N
 P = 128
-T = 8
+T = 16
 CHUNKS = M // (P * T)
-GROUPS = 2 * CHUNKS
+HALVES = 2 * CHUNKS
+GROUPS = 4 * CHUNKS
 
 
 def tile_classlayer_t_kernel(tc, x, weight, out):
@@ -43,12 +44,13 @@ def tile_classlayer_t_kernel(tc, x, weight, out):
         for h in range(2):
             nc.sync.dma_start(out=w_sb[:, h, :], in_=weight[P * h:P * (h + 1), :])
         xs = []
-        for c in range(CHUNKS):
-            xs.append(big.tile([P, T, K], BF16, tag="xo", name="x%d" % c))
+        for c in range(HALVES):
+            xs.append(big.tile([P, 8, K], BF16, tag="xo", name="x%d" % c))
         cuts = {0: [(0, 2), (2, 4), (4, 8)], 1: [(0, 4), (4, 8)]}
-        for c in range(CHUNKS):
+        for c in range(HALVES):
+            t0 = 8 * (c % 2)
             for (a, b) in cuts.get(c, [(0, 8)]):
-                nc.sync.dma_start(out=xs[c][:, a:b, :], in_=xv[c][:, a:b, :])
+                nc.sync.dma_start(out=xs[c][:, a:b, :], in_=xv[c // 2][:, t0 + a:t0 + b, :])
 
         junk = const.tile([P, 2, K], BF16, name="junk")
         absum = const.tile([P, 2], F32, name="absum")
@@ -121,7 +123,7 @@ def tile_classlayer_t_kernel(tc, x, weight, out):
                 state[("acc", i, b)] = acc
 
         def leave(i, b, eng=None):
-            c, hf = divmod(i, 2)
+            c, hf = divmod(i, 4)
             if ("o", c) not in state:
                 state[("o", c)] = o_pool.tile([P, T, N], F32, tag="o", name="o%d" % c)
             t0 = 4 * hf + 2 * b
@@ -135,9 +137,11 @@ def tile_classlayer_t_kernel(tc, x, weight, out):
             nc.sync.dma_start(out=ov[c][:, a:b, :], in_=state[("o", c)][:, a:b, :])
 
         def store(i):
-            c, hf = divmod(i, 2)
-            if hf == 1:
+            c, hf = divmod(i, 4)
+            if c < CHUNKS - 1 and hf == 3:
                 store_rows(c, 0, T)
+            if c == CHUNKS - 1 and hf == 1:
+                store_rows(c, 0, 8)
 
         def w_transposes(h):
             wt = acc_pool.tile([P, 4, P], F32, tag="acc", name="wt")
@@ -190,9 +194,9 @@ def tile_classlayer_t_kernel(tc, x, weight, out):
         quantise(last, 1)
         leave(last - 1, 0, "s")
         leave(last - 1, 1, "s")
-        store_rows(CHUNKS - 1, 0, 4)
+        store_rows(CHUNKS - 1, 8, 12)
         passes(last)
         leave(last, 0, "s")
-        store_rows(CHUNKS - 1, 4, 6)
+        store_rows(CHUNKS - 1, 12, 14)
         leave(last, 1)
-        store_rows(CHUNKS - 1, 6, 8)
+        store_rows(CHUNKS - 1, 14, 16)

@@ -15,20 +15,19 @@ AX = mybir.AxisListType
 M, K, N = 8192, 1024, 256
 FLOPS = 2 * M * K * N
 P = 128
-T = 16
-CHUNKS = M // (P * T)
-HALVES = 2 * CHUNKS
-GROUPS = 4 * CHUNKS
+T = M // P
+GROUPS = T // 4
+X_TILE = 16
+O_TILE = 32
 
 
 def tile_classlayer_t_kernel(tc, x, weight, out):
     nc = tc.nc
-    xv = x.rearrange("(c p t) k -> c p t k", p=P, t=T)
-    ov = out.rearrange("(c p t) n -> c p t n", p=P, t=T)
+    xv = x.rearrange("(p t) k -> p t k", t=T)
+    ov = out.rearrange("(p t) n -> p t n", t=T)
     with ExitStack() as ctx:
         const = ctx.enter_context(tc.tile_pool(name="const", bufs=1))
         big = ctx.enter_context(tc.tile_pool(name="big", bufs=5))
-        o_pool = ctx.enter_context(tc.tile_pool(name="outs", bufs=CHUNKS))
         grp_pool = ctx.enter_context(tc.tile_pool(name="grp", bufs=3))
         code_pool = ctx.enter_context(tc.tile_pool(name="code", bufs=4))
         xt_pool = ctx.enter_context(tc.psum_pool(name="xtp", bufs=4))
@@ -44,13 +43,13 @@ def tile_classlayer_t_kernel(tc, x, weight, out):
         for h in range(2):
             nc.sync.dma_start(out=w_sb[:, h, :], in_=weight[P * h:P * (h + 1), :])
         xs = []
-        for c in range(HALVES):
-            xs.append(big.tile([P, 8, K], BF16, tag="xo", name="x%d" % c))
-        cuts = {0: [(0, 2), (2, 4), (4, 8)], 1: [(0, 4), (4, 8)]}
-        for c in range(HALVES):
-            t0 = 8 * (c % 2)
-            for (a, b) in cuts.get(c, [(0, 8)]):
-                nc.sync.dma_start(out=xs[c][:, a:b, :], in_=xv[c // 2][:, t0 + a:t0 + b, :])
+        for c in range(T // X_TILE):
+            xs.append(big.tile([P, X_TILE, K], BF16, tag="xo", name="x%d" % c))
+        cuts = {0: [(0, 2), (2, 4), (4, 8), (8, 16)], 1: [(0, 8), (8, 16)]}
+        for c in range(T // X_TILE):
+            t0 = X_TILE * c
+            for (a, b) in cuts.get(c, [(0, X_TILE)]):
+                nc.sync.dma_start(out=xs[c][:, a:b, :], in_=xv[:, t0 + a:t0 + b, :])
 
         junk = const.tile([P, 2, K], BF16, name="junk")
         absum = const.tile([P, 2], F32, name="absum")
@@ -73,7 +72,7 @@ def tile_classlayer_t_kernel(tc, x, weight, out):
         state = {}
 
         def transposes(i, mts):
-            c, hf = divmod(i, 2)
+            c, hf = divmod(i, X_TILE // 4)
             xw = xs[c][:].bitcast(F32)
             for mt in mts:
                 xt = xt_pool.tile([P, 4, P], F32, tag="xt", name="xt")
@@ -123,9 +122,9 @@ def tile_classlayer_t_kernel(tc, x, weight, out):
                 state[("acc", i, b)] = acc
 
         def leave(i, b, eng=None):
-            c, hf = divmod(i, 4)
+            c, hf = divmod(i, O_TILE // 4)
             if ("o", c) not in state:
-                state[("o", c)] = o_pool.tile([P, T, N], F32, tag="o", name="o%d" % c)
+                state[("o", c)] = big.tile([P, O_TILE, N], F32, tag="xo", name="o%d" % c)
             t0 = 4 * hf + 2 * b
             dst = state[("o", c)][:, t0:t0 + 2, :].rearrange("p t n -> p (t n)")
             if eng == "s":
@@ -133,15 +132,14 @@ def tile_classlayer_t_kernel(tc, x, weight, out):
             else:
                 nc.vector.tensor_copy(out=dst, in_=state[("acc", i, b)][:])
 
-        def store_rows(c, a, b):
-            nc.sync.dma_start(out=ov[c][:, a:b, :], in_=state[("o", c)][:, a:b, :])
+        def store_rows(a, b):
+            c = a // O_TILE
+            nc.sync.dma_start(out=ov[:, a:b, :], in_=state[("o", c)][:, a - O_TILE * c:b - O_TILE * c, :])
 
         def store(i):
-            c, hf = divmod(i, 4)
-            if c < CHUNKS - 1 and hf == 3:
-                store_rows(c, 0, T)
-            if c == CHUNKS - 1 and hf == 1:
-                store_rows(c, 0, 8)
+            for (a, b) in ((0, 32), (32, 48), (48, 56)):
+                if b == 4 * (i + 1):
+                    store_rows(a, b)
 
         def w_transposes(h):
             wt = acc_pool.tile([P, 4, P], F32, tag="acc", name="wt")
@@ -194,9 +192,9 @@ def tile_classlayer_t_kernel(tc, x, weight, out):
         quantise(last, 1)
         leave(last - 1, 0, "s")
         leave(last - 1, 1, "s")
-        store_rows(CHUNKS - 1, 8, 12)
+        store_rows(56, 60)
         passes(last)
         leave(last, 0, "s")
-        store_rows(CHUNKS - 1, 12, 14)
+        store_rows(60, 62)
         leave(last, 1)
-        store_rows(CHUNKS - 1, 14, 16)
+        store_rows(62, 64)

@@ -40,12 +40,11 @@ def tile_classlayer_t_kernel(tc, x, weight, out):
         nc.vector.memset(ones[:], 1.0 / (N * K))
 
         w_sb = const.tile([P, 2, K], BF16, name="w_sb")
-        for h in range(2):
-            nc.sync.dma_start(out=w_sb[:, h, :], in_=weight[P * h:P * (h + 1), :])
+        nc.sync.dma_start(out=w_sb[:], in_=weight.rearrange("(h p) k -> p h k", p=P))
         xs = []
         for c in range(T // X_TILE):
             xs.append(big.tile([P, X_TILE, K], BF16, tag="xo", name="x%d" % c))
-        cuts = {0: [(0, 2), (2, 4), (4, 8), (8, 16)], 1: [(0, 8), (8, 16)]}
+        cuts = {0: [(0, 4), (4, 8), (8, 16)], 1: [(0, 8), (8, 16)], 2: [(0, 8), (8, 16)]}
         for c in range(T // X_TILE):
             t0 = X_TILE * c
             for (a, b) in cuts.get(c, [(0, X_TILE)]):
@@ -192,9 +191,8 @@ def tile_classlayer_t_kernel(tc, x, weight, out):
         quantise(last, 1)
         leave(last - 1, 0, "s")
         leave(last - 1, 1, "s")
-        store_rows(56, 60)
         passes(last)
         leave(last, 0, "s")
-        store_rows(60, 62)
+        store_rows(56, 62)
         leave(last, 1)
         store_rows(62, 64)

from contextlib import ExitStack

import concourse.mybir as mybir
from concourse.masks import make_identity

F32 = mybir.dt.float32
BF16 = mybir.dt.bfloat16
U32 = mybir.dt.uint32
U8 = mybir.dt.uint8
FP8X4 = mybir.dt.float8_e4m3fn_x4
ALU = mybir.AluOpType
ACT = mybir.ActivationFunctionType
AX = mybir.AxisListType

M, K, N = 8192, 1024, 256
FLOPS = 2 * M * K * N
P = 128
T = M // P
GROUPS = T // 4
X_TILE = 16
O_TILE = 32


def tile_classlayer_t_kernel(tc, x, weight, out):
    nc = tc.nc
    xv = x.rearrange("(p t) k -> p t k", t=T)
    ov = out.rearrange("(p t) n -> p t n", t=T)
    with ExitStack() as ctx:
        const = ctx.enter_context(tc.tile_pool(name="const", bufs=1))
        big = ctx.enter_context(tc.tile_pool(name="big", bufs=5))
        grp_pool = ctx.enter_context(tc.tile_pool(name="grp", bufs=3))
        code_pool = ctx.enter_context(tc.tile_pool(name="code", bufs=4))
        xt_pool = ctx.enter_context(tc.psum_pool(name="xtp", bufs=4))
        acc_pool = ctx.enter_context(tc.psum_pool(name="accp", bufs=4))
        ctx.enter_context(tc.manual_schedule())

        ident = const.tile([P, P], F32, name="ident")
        make_identity(nc, ident[:])
        ones = const.tile([P, P], F32, name="ones")
        nc.vector.memset(ones[:], 1.0 / (N * K))

        w_sb = const.tile([P, 2, K], BF16, name="w_sb")
        nc.sync.dma_start(out=w_sb[:], in_=weight.rearrange("(h p) k -> p h k", p=P))
        xs = []
        for c in range(T // X_TILE):
            xs.append(big.tile([P, X_TILE, K], BF16, tag="xo", name="x%d" % c))
        cuts = {0: [(0, 4), (4, 8), (8, 16)], 1: [(0, 8), (8, 16)], 2: [(0, 8), (8, 16)]}
        for c in range(T // X_TILE):
            t0 = X_TILE * c
            for (a, b) in cuts.get(c, [(0, X_TILE)]):
                nc.sync.dma_start(out=xs[c][:, a:b, :], in_=xv[:, t0 + a:t0 + b, :])

        junk = const.tile([P, 2, K], BF16, name="junk")
        absum = const.tile([P, 2], F32, name="absum")
        neg = const.tile([P, 2, K], BF16, name="neg")
        pos = const.tile([P, 2, K], BF16, name="pos")
        sgn = const.tile([P, 2, K], BF16, name="sgn")
        for h in range(2):
            nc.scalar.activation(out=junk[:, h, :], in_=w_sb[:, h, :], func=ACT.Abs,
                                 accum_out=absum[:, h:h + 1])
            nc.vector.tensor_single_scalar(out=neg[:, h, :], in_=w_sb[:, h, :], scalar=0.0, op=ALU.is_lt)
            nc.vector.tensor_single_scalar(out=pos[:, h, :], in_=w_sb[:, h, :], scalar=0.0, op=ALU.is_gt)
            nc.vector.tensor_tensor(out=sgn[:, h, :], in0=pos[:, h, :], in1=neg[:, h, :], op=ALU.subtract)
        sgn_w = sgn[:].bitcast(F32)

        gwt = const.tile([P, 2, N, 4], BF16, name="gwt", align_bytes=64)
        wcodes = const.tile([P, 2 * N], U32, name="wcodes", align_bytes=64)
        wscales = const.tile([P, 2 * N], U8, name="wscales", align_bytes=64)
        scale = const.tile([P, 1], F32, name="scale")

        state = {}

        def transposes(i, mts):
            c, hf = divmod(i, X_TILE // 4)
            xw = xs[c][:].bitcast(F32)
            for mt in mts:
                xt = xt_pool.tile([P, 4, P], F32, tag="xt", name="xt")
                for j in range(4):
                    nc.tensor.transpose(xt[:, j, :], xw[:, 4 * hf + mt, P * j:P * (j + 1)], ident[:])
                state[("xt", i, mt)] = xt

        def copies(i, mts, eng=None):
            if ("grp", i) not in state:
                state[("grp", i)] = grp_pool.tile([P, 4096], BF16, tag="grp", name="grp", align_bytes=64)
            gw = state[("grp", i)][:].bitcast(F32)
            for mt in mts:
                dst = gw[:, 512 * mt:512 * (mt + 1)].rearrange("p (g m u) -> p g m u", g=2, u=2)
                src = state[("xt", i, mt)][:].rearrange("p (g u) m -> p g m u", u=2)
                if eng == "v":
                    nc.vector.tensor_copy(out=dst, in_=src)
                else:
                    nc.scalar.copy(out=dst, in_=src)

        def quantise(i, a):
            if ("codes", i) not in state:
                state[("codes", i)] = code_pool.tile([P, 1024], U32, tag="codes", name="codes", align_bytes=64)
                state[("scales", i)] = code_pool.tile([P, 1024], U8, tag="scales", name="scales", align_bytes=64)
            nc.vector.quantize_mx(
                out=state[("codes", i)][:, 512 * a:512 * (a + 1)].bitcast(FP8X4),
                scales=state[("scales", i)][:, 512 * a:512 * (a + 1)],
                in_=state[("grp", i)][:, 2048 * a:2048 * (a + 1)],
            )

        def passes(i):
            codes = state[("codes", i)]
            scales = state[("scales", i)]
            for b in range(2):
                acc = acc_pool.tile([P, 512], F32, tag="acc", name="acc")
                for s in range(2):
                    for g in range(2):
                        col = (2 * (2 * b + s) + g) * P
                        nc.tensor.matmul_mx(
                            out=acc[:, N * s:N * (s + 1)],
                            lhsT=codes[:, col:col + P].bitcast(FP8X4),
                            lhsT_scale=scales[:, col:col + P],
                            rhs=wcodes[:, N * g:N * (g + 1)].bitcast(FP8X4),
                            rhs_scale=wscales[:, N * g:N * (g + 1)],
                            start=(g == 0),
                            stop=(g == 1),
                        )
                state[("acc", i, b)] = acc

        def leave(i, b, eng=None):
            c, hf = divmod(i, O_TILE // 4)
            if ("o", c) not in state:
                state[("o", c)] = big.tile([P, O_TILE, N], F32, tag="xo", name="o%d" % c)
            t0 = 4 * hf + 2 * b
            dst = state[("o", c)][:, t0:t0 + 2, :].rearrange("p t n -> p (t n)")
            if eng == "s":
                nc.scalar.copy(out=dst, in_=state[("acc", i, b)][:])
            else:
                nc.vector.tensor_copy(out=dst, in_=state[("acc", i, b)][:])

        def store_rows(a, b):
            c = a // O_TILE
            nc.sync.dma_start(out=ov[:, a:b, :], in_=state[("o", c)][:, a - O_TILE * c:b - O_TILE * c, :])

        def store(i):
            for (a, b) in ((0, 32), (32, 48), (48, 56)):
                if b == 4 * (i + 1):
                    store_rows(a, b)

        def w_transposes(h):
            wt = acc_pool.tile([P, 4, P], F32, tag="acc", name="wt")
            for j in range(4):
                nc.tensor.transpose(wt[:, j, :], sgn_w[:, h, P * j:P * (j + 1)], ident[:])
            state[("wt", h)] = wt

        def w_scaled(h, g):
            src = state[("wt", h)][:].bitcast(BF16).rearrange("p (g u) (n e) -> p g n u e", u=2, e=2)[:, g]
            dst = gwt[:, g, P * h:P * (h + 1), :].rearrange("p n (u e) -> p n u e", e=2)
            if h == 0:
                nc.vector.tensor_scalar(out=dst, in0=src, scalar1=scale[:, 0:1], scalar2=None, op0=ALU.mult)
            else:
                nc.scalar.activation(out=dst, in_=src, func=ACT.Copy, scale=scale[:, 0:1])

        w_transposes(0)
        transposes(0, [0, 1])
        sm = acc_pool.tile([P, 2], F32, tag="acc", name="sm")
        nc.tensor.matmul(out=sm[:], lhsT=ones[:], rhs=absum[:], start=True, stop=True)
        w_transposes(1)
        transposes(0, [2, 3])
        copies(0, [0, 1])
        nc.vector.tensor_reduce(out=scale[:], in_=sm[:], axis=AX.X, op=ALU.add)
        for g in range(2):
            w_scaled(0, g)
            w_scaled(1, g)
        nc.vector.quantize_mx(out=wcodes[:].bitcast(FP8X4), scales=wscales[:],
                              in_=gwt[:].rearrange("p g n t -> p (g n t)"))
        copies(0, [2, 3])
        quantise(0, 0)
        quantise(0, 1)

        for i in range(1, GROUPS - 1):
            transposes(i, [0, 1, 2, 3])
            copies(i, [0, 1, 2, 3])
            passes(i - 1)
            quantise(i, 0)
            leave(i - 1, 0)
            quantise(i, 1)
            leave(i - 1, 1)
            store(i - 1)

        last = GROUPS - 1
        transposes(last, [0, 1, 2, 3])
        copies(last, [0, 1])
        copies(last, [2], "v")
        copies(last, [3])
        passes(last - 1)
        quantise(last, 0)
        quantise(last, 1)
        leave(last - 1, 0, "s")
        leave(last - 1, 1, "s")
        passes(last)
        leave(last, 0, "s")
        store_rows(56, 62)
        leave(last, 1)
        store_rows(62, 64)
